import numpy as np
import ml_dtypes


def mxq(x, axis, fmt="e4m3"):
    dtype, down = {"e4m3": (ml_dtypes.float8_e4m3fn, 7), "e5m2": (ml_dtypes.float8_e5m2, 14)}[fmt]
    v = np.moveaxis(np.asarray(x, np.float32).astype(ml_dtypes.bfloat16).astype(np.float64), axis, -1)
    blocks = v.reshape(v.shape[:-1] + (-1, 32))
    amax = np.abs(blocks).max(-1, keepdims=True)
    byte = np.maximum(np.where(amax > 0, np.frexp(amax)[1] - 1 + 127, 0) - down, 1)
    scale = np.exp2(byte - 127.0)
    codes = (blocks / scale).astype(np.float32).astype(dtype).astype(np.float64)
    return np.moveaxis((codes * scale).reshape(v.shape), -1, axis)


WIDE = False


def mx_kscale(k):
    if not WIDE:
        return np.ones(k)
    levels = np.array([30, -30])
    if k % 512:
        return np.exp2(np.random.permutation(np.resize(levels, k // 32))).repeat(32)
    a = np.empty((k // 512, 16))
    for p in range(k // 512):
        a[p, :8] = np.random.permutation(np.resize(levels, 8))
        for g in range(8):
            far = levels[np.abs(levels - a[p, g]) >= 10]
            a[p, g + 8] = far[np.random.randint(len(far))]
    return np.exp2(a.ravel()).repeat(32)


BF16 = ml_dtypes.bfloat16


def bf(x):
    return np.asarray(x, np.float32).astype(BF16)


def f64(x):
    return np.asarray(x).astype(np.float64)


B, S, D, H, KV, DH, QB = 1, 1024, 1024, 16, 4, 128, 512
HALF = DH // 2
EPS = 1e-6


def rope_tables():
    inv_freq = 1.0 / (10000.0 ** (np.arange(HALF) / HALF))
    ang = np.arange(S)[:, None] * inv_freq[None, :]
    ang = np.concatenate([ang, ang], axis=-1)
    return np.sin(ang), np.cos(ang)


def rmsnorm(u, scale, shift):
    rms = np.sqrt(np.mean(u * u, axis=-1, keepdims=True) + EPS)
    return u / rms * (1.0 + scale) + shift


def apply_rope(u, sin, cos):
    rot = np.concatenate([-u[..., HALF:], u[..., :HALF]], axis=-1)
    return u * cos[None, None, :S, :] + rot * sin[None, None, :S, :]


def heads(u, n):
    return u.reshape(B, S, n, DH).transpose(0, 2, 1, 3)


def setup_inputs():
    s = mx_kscale(D)
    sin, cos = rope_tables()
    return {"x": bf(np.random.standard_normal((B, S, D)) * s),
            "sin_thetas": bf(sin), "cos_thetas": bf(cos),
            "wq": bf(np.random.standard_normal((H * DH, D)) / np.sqrt(D) / s),
            "wk": bf(np.random.standard_normal((KV * DH, D)) / np.sqrt(D) / s),
            "wv": bf(np.random.standard_normal((KV * DH, D)) * 2.0 / np.sqrt(D) / s),
            "q_scale": bf(np.random.standard_normal(DH) * 0.1), "q_shift": bf(np.random.standard_normal(DH) * 0.1),
            "k_scale": bf(np.random.standard_normal(DH) * 0.1), "k_shift": bf(np.random.standard_normal(DH) * 0.1)}


def reference(x, sin_thetas, cos_thetas, wq, wk, wv, q_scale, q_shift, k_scale, k_shift):
    xq = mxq(f64(x), 2, "e5m2")
    q = heads(xq @ mxq(f64(wq), 1, "e5m2").T, H)
    k = heads(xq @ mxq(f64(wk), 1, "e5m2").T, KV)
    v = heads(xq @ mxq(f64(wv), 1, "e5m2").T, KV)
    q = rmsnorm(q, f64(q_scale), f64(q_shift))
    k = rmsnorm(k, f64(k_scale), f64(k_shift))
    q = apply_rope(q, f64(sin_thetas), f64(cos_thetas))
    k = apply_rope(k, f64(sin_thetas), f64(cos_thetas))
    return q, k, v

@@ -1,0 +1,275 @@
+from contextlib import ExitStack
+
+import concourse.mybir as mybir
+from concourse.masks import make_identity
+
+F32 = mybir.dt.float32
+BF16 = mybir.dt.bfloat16
+U32 = mybir.dt.uint32
+U8 = mybir.dt.uint8
+E5X4 = mybir.dt.float8_e5m2_x4
+ACT = mybir.ActivationFunctionType
+ALU = mybir.AluOpType
+
+P = 128
+SEQ = 1024
+KDIM = 1024
+DH = 128
+HALF = 64
+MT = SEQ // P
+EPS = 1e-6
+FLOPS = 2 * SEQ * KDIM * 3072
+
+
+def tile_groupqueryattention_pa_kernel(
+    tc, x, sin_thetas, cos_thetas, wq, wk, wv, q_scale, q_shift, k_scale, k_shift, out_0, out_1, out_2
+):
+    nc = tc.nc
+    with ExitStack() as ctx:
+        const = ctx.enter_context(tc.tile_pool(name="const", bufs=1))
+        work = ctx.enter_context(tc.tile_pool(name="work", bufs=1))
+        psum = ctx.enter_context(tc.psum_pool(name="psum", bufs=1))
+
+        vec_rows = const.tile([P, 4 * DH], BF16, name="vec_rows")
+        nc.gpsimd.memset(vec_rows[:], 0.0)
+        for j, vec in enumerate((q_scale, q_shift, k_scale, k_shift)):
+            nc.sync.dma_start(
+                out=vec_rows[0:1, j * DH : (j + 1) * DH], in_=vec.rearrange("(o d) -> o d", o=1)
+            )
+        cos_sb = const.tile([P, MT, DH], BF16, name="cos_sb")
+        sin_sb = const.tile([P, MT, DH], BF16, name="sin_sb")
+        nc.sync.dma_start(out=cos_sb[:], in_=cos_thetas.rearrange("(p m) d -> p m d", m=MT))
+        nc.sync.dma_start(out=sin_sb[:], in_=sin_thetas.rearrange("(p m) d -> p m d", m=MT))
+
+        x_view = x[0].rearrange("(p m) k -> p m k", m=MT)
+        x_sb = []
+        w_sb = {}
+
+        def load_x(pair):
+            t = const.tile([P, 2, KDIM], BF16, name="x_sb%d" % pair)
+            nc.sync.dma_start(out=t[:], in_=x_view[:, 2 * pair : 2 * pair + 2, :])
+            x_sb.append(t)
+
+        def load_w(key, w, row0):
+            halves = []
+            for hf in range(2):
+                t = const.tile([P, 2, KDIM], BF16, name="w_sb_%s_%d" % (key, hf))
+                nc.sync.dma_start(
+                    out=t[:],
+                    in_=w[row0 + 256 * hf : row0 + 256 * (hf + 1), :].rearrange("(c p) k -> p c k", p=P),
+                )
+                halves.append(t)
+            w_sb[key] = halves
+
+        load_x(0)
+        load_w("q0", wq, 0)
+        load_x(1)
+        load_x(2)
+        load_x(3)
+        load_w("v", wv, 0)
+        load_w("q1", wq, 512)
+        load_w("q2", wq, 1024)
+        load_w("q3", wq, 1536)
+        load_w("k", wk, 0)
+
+        ident = const.tile([P, P], F32, name="ident")
+        make_identity(nc, ident[:])
+        ones = const.tile([P, P], BF16, name="ones")
+        nc.vector.memset(ones[:], 1.0)
+        warm = const.tile([P, 1], F32, name="warm")
+        nc.vector.memset(warm[:], 1.0)
+        nc.scalar.activation(out=warm[:], in_=warm[:], func=ACT.Abs_reciprocal_sqrt)
+
+        bc_ps = psum.tile([P, 512], F32, tag="tp", bufs=2, name="bc_ps")
+        nc.tensor.matmul(out=bc_ps[:], lhsT=ones[:], rhs=vec_rows[:], start=True, stop=True)
+        bc4 = bc_ps[:].rearrange("p (t s d) -> p t s d", t=2, s=2)
+        gain4 = const.tile([P, 2, 4 * HALF], F32, name="gain4")
+        shift2 = const.tile([P, 2, 4 * HALF], F32, name="shift2")
+        nc.vector.tensor_scalar_add(out=gain4[:, :, 0:64], in0=bc4[:, :, 0, 0:64], scalar1=1.0)
+        nc.vector.tensor_scalar(
+            out=gain4[:, :, 64:128], in0=bc4[:, :, 0, 64:128], scalar1=-1.0, scalar2=-1.0,
+            op0=ALU.mult, op1=ALU.add,
+        )
+        nc.vector.tensor_scalar_add(out=gain4[:, :, 128:256], in0=bc4[:, :, 0, :], scalar1=1.0)
+        nc.vector.tensor_copy(out=shift2[:, :, 0:128], in_=bc4[:, :, 1, :])
+        nc.vector.tensor_scalar_mul(out=shift2[:, :, 128:192], in0=bc4[:, :, 1, 64:128], scalar1=-1.0)
+        nc.vector.tensor_copy(out=shift2[:, :, 192:256], in_=bc4[:, :, 1, 0:64])
+
+        def over_m(ap, n_m):
+            return ap.unsqueeze(1).to_broadcast([P, n_m, ap.shape[1]])
+
+        def tab_steps(eng, tab, t):
+            return [
+                lambda: eng.tensor_tensor(out=tab[:, :, 0:64], in0=cos_sb[:, :, 0:64],
+                                          in1=over_m(gain4[:, t, 0:64], MT), op=ALU.mult),
+                lambda: eng.tensor_tensor(out=tab[:, :, 64:192], in0=sin_sb[:],
+                                          in1=over_m(gain4[:, t, 64:192], MT), op=ALU.mult),
+                lambda: eng.tensor_tensor(out=tab[:, :, 192:256], in0=cos_sb[:, :, 64:128],
+                                          in1=over_m(gain4[:, t, 192:256], MT), op=ALU.mult),
+            ]
+
+        def c_steps(eng, c_sb, c_tmp, t):
+            steps = []
+            for j in range(2):
+                ms = slice(4 * j, 4 * j + 4)
+                steps.append(lambda ms=ms: eng.tensor_tensor(
+                    out=c_sb[:, ms, :], in0=cos_sb[:, ms, :], in1=over_m(shift2[:, t, 0:128], 4), op=ALU.mult))
+                steps.append(lambda ms=ms: eng.tensor_tensor(
+                    out=c_tmp[:, ms, :], in0=sin_sb[:, ms, :], in1=over_m(shift2[:, t, 128:256], 4), op=ALU.mult))
+                steps.append(lambda ms=ms: eng.tensor_tensor(
+                    out=c_sb[:, ms, :], in0=c_sb[:, ms, :], in1=c_tmp[:, ms, :], op=ALU.add))
+            return steps
+
+        def c_to_psum(c_sb):
+            banks = []
+            for j in range(2):
+                cps = psum.tile([P, 512], F32, tag="cps", bufs=2, name="cps")
+                nc.tensor.matmul(
+                    out=cps[:], lhsT=ident[:],
+                    rhs=c_sb[:, 4 * j : 4 * j + 4, :].rearrange("p m d -> p (m d)"),
+                    start=True, stop=True,
+                )
+                banks.append(cps)
+            return banks
+
+        tab_q = const.tile([P, MT, 4 * HALF], F32, name="tab_q")
+        tab_k = const.tile([P, MT, 4 * HALF], F32, name="tab_k")
+        c_q = const.tile([P, MT, DH], F32, name="c_q")
+        c_k = const.tile([P, MT, DH], F32, name="c_k")
+        c_tmp = const.tile([P, MT, DH], F32, name="c_tmp")
+        for step in tab_steps(nc.vector, tab_q, 0):
+            step()
+        for step in c_steps(nc.gpsimd, c_q, c_tmp, 0):
+            step()
+        cps_q = c_to_psum(c_q)
+        late_steps = tab_steps(nc.gpsimd, tab_k, 1) + c_steps(nc.gpsimd, c_k, c_tmp, 1)
+
+        def prep(name, srcs, widths):
+            rows = 256 * len(srcs)
+            grouped = work.tile([P, 8 * rows], BF16, tag="grouped", bufs=3, name="grouped", align_bytes=64)
+            gw = grouped[:].bitcast(F32)
+            codes = const.tile([P, 2 * rows], U32, name="codes_" + name, align_bytes=64)
+            scales = const.tile([P, 2 * rows], U8, name="scales_" + name, align_bytes=64)
+            for g in range(2):
+                for s, src in enumerate(srcs):
+                    tp = psum.tile([P, 2, 256], F32, tag="tp", bufs=2, name="tp")
+                    for c in range(2):
+                        words = src[:, c, :].bitcast(F32)
+                        for u in range(2):
+                            nc.tensor.transpose(
+                                tp[:, u, c * P : (c + 1) * P],
+                                words[:, 256 * g + u : 256 * (g + 1) : 2],
+                                ident[:],
+                            )
+                    w0 = (g * rows + s * 256) * 2
+                    nc.scalar.copy(
+                        out=gw[:, w0 : w0 + 512].rearrange("p (r u) -> p r u", u=2),
+                        in_=tp[:].rearrange("p u r -> p r u"),
+                    )
+            for c0 in range(0, 2 * rows, widths):
+                nc.vector.quantize_mx(
+                    out=codes[:, c0 : c0 + widths].bitcast(E5X4),
+                    scales=scales[:, c0 : c0 + widths],
+                    in_=grouped[:, 4 * c0 : 4 * (c0 + widths)],
+                )
+            return codes, scales
+
+        xq = {}
+        wqz = {}
+
+        def prep_x(pair, widths=512):
+            xq[pair] = prep("x%d" % pair, [x_sb[pair]], widths)
+
+        def prep_w(key, widths=1024):
+            wqz[key] = prep("w" + key, w_sb[key], widths)
+
+        def mx_bank(m, key):
+            acc = psum.tile([P, 512], F32, tag="acc", bufs=4, name="acc")
+            pair, half = divmod(m, 2)
+            xc, xs = xq[pair]
+            wc, ws = wqz[key]
+            for g in range(2):
+                xcols = slice(g * 256 + half * P, g * 256 + (half + 1) * P)
+                wcols = slice(g * 512, (g + 1) * 512)
+                nc.tensor.matmul_mx(
+                    out=acc[:],
+                    lhsT=xc[:, xcols].bitcast(E5X4), lhsT_scale=xs[:, xcols],
+                    rhs=wc[:, wcols].bitcast(E5X4), rhs_scale=ws[:, wcols],
+                    start=(g == 0), stop=(g == 1),
+                )
+            return acc
+
+        def out_view(out, h0):
+            return out[0, h0 : h0 + 4, :, :].rearrange("h (p m) d -> p h m d", m=MT)
+
+        state = {"late": 0}
+
+        def normed_bank(m, key, tab, cps, out, h0, group):
+            acc = mx_bank(m, key)
+            ss = work.tile([P, 4], F32, tag="ss", bufs=4, name="ss")
+            junk = work.tile([P, DH], F32, tag="junk", bufs=2, name="junk")
+            for h in range(4):
+                nc.scalar.activation(out=junk[:], in_=acc[:, h * DH : (h + 1) * DH], func=ACT.Square,
+                                     accum_out=ss[:, h : h + 1])
+            rinv = work.tile([P, 4], F32, tag="rinv", bufs=4, name="rinv")
+            nc.scalar.activation(out=rinv[:], in_=ss[:], func=ACT.Abs_reciprocal_sqrt, bias=EPS, scale=1.0 / DH)
+            prod = work.tile([P, 4, 4 * HALF], F32, tag="prod", bufs=4, name="prod")
+            nc.vector.tensor_tensor(
+                out=prod[:].rearrange("p h (k d) -> p h k d", k=2),
+                in0=acc[:].rearrange("p (h d) -> p h d", h=4).unsqueeze(2).to_broadcast([P, 4, 2, DH]),
+                in1=tab[:, m, :].rearrange("p (k d) -> p k d", k=2).unsqueeze(1).to_broadcast([P, 4, 2, DH]),
+                op=ALU.mult,
+            )
+            prod4 = prod[:].rearrange("p h (k e) -> p h k e", k=4)
+            rot = work.tile([P, 4, DH], F32, tag="rot", bufs=4, name="rot")
+            nc.gpsimd.tensor_tensor(
+                out=rot[:].rearrange("p h (t e) -> p h t e", t=2),
+                in0=prod4[:, :, 0:4:3, :], in1=prod4[:, :, 1:3, :], op=ALU.add,
+            )
+            mm = m % group
+            if mm == 0:
+                state["o"] = work.tile([P, 4, group, DH], F32, tag="o", bufs=4, name="o")
+            o = state["o"]
+            for h in range(4):
+                nc.vector.scalar_tensor_tensor(
+                    out=o[:, h, mm, :], in0=rot[:, h, :], scalar=rinv[:, h : h + 1],
+                    in1=cps[m // 4][:, (m % 4) * DH : (m % 4 + 1) * DH],
+                    op0=ALU.mult, op1=ALU.add,
+                )
+            if mm == group - 1:
+                nc.sync.dma_start(out=out_view(out, h0)[:, :, m - mm : m + 1, :], in_=o[:])
+
+        def plain_bank(m):
+            acc = mx_bank(m, "v")
+            mm = m % 2
+            if mm == 0:
+                state["ov"] = work.tile([P, 4, 2, DH], F32, tag="ov", bufs=2, name="ov")
+            ov = state["ov"]
+            nc.scalar.copy(out=ov[:, :, mm, :], in_=acc[:].rearrange("p (h d) -> p h d", h=4))
+            if mm == 1:
+                nc.sync.dma_start(out=out_view(out_2, 0)[:, :, m - 1 : m + 1, :], in_=ov[:])
+
+        prep_x(0, 256)
+        prep_w("q0", 256)
+        prep_x(1)
+        main = ["q0", "q1", "q2", "q3", "k"]
+        extra = {(0, 1): lambda: prep_x(2), (0, 3): lambda: prep_x(3), (0, 4): lambda: prep_w("q1"),
+                 (0, 6): lambda: prep_w("v")}
+        cps_now = cps_q
+        for ci, key in enumerate(main):
+            if key == "k":
+                cps_now = c_to_psum(c_k)
+            for m in range(MT):
+                if key == "k":
+                    normed_bank(m, key, tab_k, cps_now, out_1, 0, 2 if m < 6 else 1)
+                else:
+                    normed_bank(m, key, tab_q, cps_now, out_0, 4 * ci, 2)
+                if (ci, m) in extra:
+                    extra[(ci, m)]()
+                if ci >= 1 and m == 2 and ci + 1 < len(main):
+                    prep_w(main[ci + 1])
+                if ci >= 1 and m in (1, 5):
+                    plain_bank(2 * (ci - 1) + (m - 1) // 4)
+                if m % 2 == 0 and (ci, m) >= (0, 2) and state["late"] < len(late_steps):
+                    late_steps[state["late"]]()
+                    state["late"] = state["late"] + 1

@@ -91,9 +91,6 @@ def tile_groupqueryattention_pa_kernel(
             op0=ALU.mult, op1=ALU.add,
         )
         nc.vector.tensor_scalar_add(out=gain4[:, :, 128:256], in0=bc4[:, :, 0, :], scalar1=1.0)
-        nc.vector.tensor_copy(out=shift2[:, :, 0:128], in_=bc4[:, :, 1, :])
-        nc.vector.tensor_scalar_mul(out=shift2[:, :, 128:192], in0=bc4[:, :, 1, 64:128], scalar1=-1.0)
-        nc.vector.tensor_copy(out=shift2[:, :, 192:256], in_=bc4[:, :, 1, 0:64])
 
         def over_m(ap, n_m):
             return ap.unsqueeze(1).to_broadcast([P, n_m, ap.shape[1]])
@@ -139,6 +136,9 @@ def tile_groupqueryattention_pa_kernel(
         c_tmp = const.tile([P, MT, DH], F32, name="c_tmp")
         for step in tab_steps(nc.vector, tab_q, 0):
             step()
+        nc.vector.tensor_copy(out=shift2[:, :, 0:128], in_=bc4[:, :, 1, :])
+        nc.vector.tensor_scalar_mul(out=shift2[:, :, 128:192], in0=bc4[:, :, 1, 64:128], scalar1=-1.0)
+        nc.vector.tensor_copy(out=shift2[:, :, 192:256], in_=bc4[:, :, 1, 0:64])
         for step in c_steps(nc.gpsimd, c_q, c_tmp, 0):
             step()
         cps_q = c_to_psum(c_q)
@@ -150,8 +150,8 @@ def tile_groupqueryattention_pa_kernel(
             gw = grouped[:].bitcast(F32)
             codes = const.tile([P, 2 * rows], U32, name="codes_" + name, align_bytes=64)
             scales = const.tile([P, 2 * rows], U8, name="scales_" + name, align_bytes=64)
-            for g in range(2):
-                for s, src in enumerate(srcs):
+            for s, src in enumerate(srcs):
+                for g in range(2):
                     tp = psum.tile([P, 2, 256], F32, tag="tp", bufs=2, name="tp")
                     for c in range(2):
                         words = src[:, c, :].bitcast(F32)
@@ -216,8 +216,8 @@ def tile_groupqueryattention_pa_kernel(
             prod = work.tile([P, 4, 4 * HALF], F32, tag="prod", bufs=4, name="prod")
             nc.vector.tensor_tensor(
                 out=prod[:].rearrange("p h (k d) -> p h k d", k=2),
-                in0=acc[:].rearrange("p (h d) -> p h d", h=4).unsqueeze(2).to_broadcast([P, 4, 2, DH]),
-                in1=tab[:, m, :].rearrange("p (k d) -> p k d", k=2).unsqueeze(1).to_broadcast([P, 4, 2, DH]),
+                in0=tab[:, m, :].rearrange("p (k d) -> p k d", k=2).unsqueeze(1).to_broadcast([P, 4, 2, DH]),
+                in1=acc[:].rearrange("p (h d) -> p h d", h=4).unsqueeze(2).to_broadcast([P, 4, 2, DH]),
                 op=ALU.mult,
             )
             prod4 = prod[:].rearrange("p h (k e) -> p h k e", k=4)
@@ -230,12 +230,15 @@ def tile_groupqueryattention_pa_kernel(
             if mm == 0:
                 state["o"] = work.tile([P, 4, group, DH], F32, tag="o", bufs=4, name="o")
             o = state["o"]
+            scaled = work.tile([P, 4, DH], F32, tag="scaled", bufs=4, name="scaled")
             for h in range(4):
-                nc.vector.scalar_tensor_tensor(
-                    out=o[:, h, mm, :], in0=rot[:, h, :], scalar=rinv[:, h : h + 1],
-                    in1=cps[m // 4][:, (m % 4) * DH : (m % 4 + 1) * DH],
-                    op0=ALU.mult, op1=ALU.add,
-                )
+                nc.scalar.activation(out=scaled[:, h, :], in_=rot[:, h, :], func=ACT.Copy,
+                                     scale=rinv[:, h : h + 1])
+            nc.vector.tensor_tensor(
+                out=o[:, :, mm, :], in0=scaled[:],
+                in1=cps[m // 4][:, (m % 4) * DH : (m % 4 + 1) * DH].unsqueeze(1).to_broadcast([P, 4, DH]),
+                op=ALU.add,
+            )
             if mm == group - 1:
                 nc.sync.dma_start(out=out_view(out, h0)[:, :, m - mm : m + 1, :], in_=o[:])
 

@@ -230,15 +230,12 @@ def tile_groupqueryattention_pa_kernel(
             if mm == 0:
                 state["o"] = work.tile([P, 4, group, DH], F32, tag="o", bufs=4, name="o")
             o = state["o"]
-            scaled = work.tile([P, 4, DH], F32, tag="scaled", bufs=4, name="scaled")
             for h in range(4):
-                nc.scalar.activation(out=scaled[:, h, :], in_=rot[:, h, :], func=ACT.Copy,
-                                     scale=rinv[:, h : h + 1])
-            nc.vector.tensor_tensor(
-                out=o[:, :, mm, :], in0=scaled[:],
-                in1=cps[m // 4][:, (m % 4) * DH : (m % 4 + 1) * DH].unsqueeze(1).to_broadcast([P, 4, DH]),
-                op=ALU.add,
-            )
+                nc.vector.scalar_tensor_tensor(
+                    out=o[:, h, mm, :], in0=rot[:, h, :], scalar=rinv[:, h : h + 1],
+                    in1=cps[m // 4][:, (m % 4) * DH : (m % 4 + 1) * DH],
+                    op0=ALU.mult, op1=ALU.add,
+                )
             if mm == group - 1:
                 nc.sync.dma_start(out=out_view(out, h0)[:, :, m - mm : m + 1, :], in_=o[:])
 

@@ -19,6 +19,7 @@ HALF = 64
 MT = SEQ // P
 EPS = 1e-6
 FLOPS = 2 * SEQ * KDIM * 3072
+OFFLOAD_EVERY = 6
 
 
 def tile_groupqueryattention_pa_kernel(
@@ -38,8 +39,6 @@ def tile_groupqueryattention_pa_kernel(
             )
         cos_sb = const.tile([P, MT, DH], BF16, name="cos_sb")
         sin_sb = const.tile([P, MT, DH], BF16, name="sin_sb")
-        nc.sync.dma_start(out=cos_sb[:], in_=cos_thetas.rearrange("(p m) d -> p m d", m=MT))
-        nc.sync.dma_start(out=sin_sb[:], in_=sin_thetas.rearrange("(p m) d -> p m d", m=MT))
 
         x_view = x[0].rearrange("(p m) k -> p m k", m=MT)
         x_sb = []
@@ -63,6 +62,8 @@ def tile_groupqueryattention_pa_kernel(
 
         load_x(0)
         load_w("q0", wq, 0)
+        nc.sync.dma_start(out=cos_sb[:], in_=cos_thetas.rearrange("(p m) d -> p m d", m=MT))
+        nc.sync.dma_start(out=sin_sb[:], in_=sin_thetas.rearrange("(p m) d -> p m d", m=MT))
         load_x(1)
         load_x(2)
         load_x(3)
@@ -74,6 +75,8 @@ def tile_groupqueryattention_pa_kernel(
 
         ident = const.tile([P, P], F32, name="ident")
         make_identity(nc, ident[:])
+        ident_bf = const.tile([P, P], BF16, name="ident_bf")
+        make_identity(nc, ident_bf[:])
         ones = const.tile([P, P], BF16, name="ones")
         nc.vector.memset(ones[:], 1.0)
         warm = const.tile([P, 1], F32, name="warm")
@@ -91,41 +94,48 @@ def tile_groupqueryattention_pa_kernel(
             op0=ALU.mult, op1=ALU.add,
         )
         nc.vector.tensor_scalar_add(out=gain4[:, :, 128:256], in0=bc4[:, :, 0, :], scalar1=1.0)
+        nc.vector.tensor_copy(out=shift2[:, :, 0:128], in_=bc4[:, :, 1, :])
+        nc.vector.tensor_scalar_mul(out=shift2[:, :, 128:192], in0=bc4[:, :, 1, 64:128], scalar1=-1.0)
+        nc.vector.tensor_copy(out=shift2[:, :, 192:256], in_=bc4[:, :, 1, 0:64])
+        dmat = const.tile([P, 4, DH], BF16, name="dmat")
+        nc.vector.tensor_tensor(
+            out=dmat[:], in0=ident[:].unsqueeze(1).to_broadcast([P, 4, DH]),
+            in1=shift2[:].rearrange("p t (j d) -> p (t j) d", j=2), op=ALU.mult,
+        )
 
         def over_m(ap, n_m):
             return ap.unsqueeze(1).to_broadcast([P, n_m, ap.shape[1]])
 
-        def tab_steps(eng, tab, t):
+        def tab_steps(eng, tab, t, m0, m1):
+            ms = slice(m0, m1)
             return [
-                lambda: eng.tensor_tensor(out=tab[:, :, 0:64], in0=cos_sb[:, :, 0:64],
-                                          in1=over_m(gain4[:, t, 0:64], MT), op=ALU.mult),
-                lambda: eng.tensor_tensor(out=tab[:, :, 64:192], in0=sin_sb[:],
-                                          in1=over_m(gain4[:, t, 64:192], MT), op=ALU.mult),
-                lambda: eng.tensor_tensor(out=tab[:, :, 192:256], in0=cos_sb[:, :, 64:128],
-                                          in1=over_m(gain4[:, t, 192:256], MT), op=ALU.mult),
+                lambda: eng.tensor_tensor(out=tab[:, ms, 0:64], in0=cos_sb[:, ms, 0:64],
+                                          in1=over_m(gain4[:, t, 0:64], m1 - m0), op=ALU.mult),
+                lambda: eng.tensor_tensor(out=tab[:, ms, 64:192], in0=sin_sb[:, ms, :],
+                                          in1=over_m(gain4[:, t, 64:192], m1 - m0), op=ALU.mult),
+                lambda: eng.tensor_tensor(out=tab[:, ms, 192:256], in0=cos_sb[:, ms, 64:128],
+                                          in1=over_m(gain4[:, t, 192:256], m1 - m0), op=ALU.mult),
             ]
 
-        def c_steps(eng, c_sb, c_tmp, t):
-            steps = []
-            for j in range(2):
-                ms = slice(4 * j, 4 * j + 4)
-                steps.append(lambda ms=ms: eng.tensor_tensor(
-                    out=c_sb[:, ms, :], in0=cos_sb[:, ms, :], in1=over_m(shift2[:, t, 0:128], 4), op=ALU.mult))
-                steps.append(lambda ms=ms: eng.tensor_tensor(
-                    out=c_tmp[:, ms, :], in0=sin_sb[:, ms, :], in1=over_m(shift2[:, t, 128:256], 4), op=ALU.mult))
-                steps.append(lambda ms=ms: eng.tensor_tensor(
-                    out=c_sb[:, ms, :], in0=c_sb[:, ms, :], in1=c_tmp[:, ms, :], op=ALU.add))
-            return steps
+        def trig_transposed():
+            trig_t = const.tile([P, 2, MT, P], BF16, name="trig_t")
+            for j, src in enumerate((cos_sb, sin_sb)):
+                tps = psum.tile([P, MT, P], BF16, tag="acc", bufs=4, name="tps")
+                for m in range(MT):
+                    nc.tensor.transpose(tps[:, m, :], src[:, m, :], ident_bf[:])
+                nc.scalar.copy(out=trig_t[:, j, :, :], in_=tps[:])
+            return trig_t
 
-        def c_to_psum(c_sb):
+        def c_tables(trig_t, t, c_sb):
             banks = []
             for j in range(2):
-                cps = psum.tile([P, 512], F32, tag="cps", bufs=2, name="cps")
-                nc.tensor.matmul(
-                    out=cps[:], lhsT=ident[:],
-                    rhs=c_sb[:, 4 * j : 4 * j + 4, :].rearrange("p m d -> p (m d)"),
-                    start=True, stop=True,
-                )
+                cps = psum.tile([P, 4, DH], F32, tag="cps", bufs=2, name="cps")
+                for i in range(4):
+                    nc.tensor.matmul(out=cps[:, i, :], lhsT=trig_t[:, 0, 4 * j + i, :], rhs=dmat[:, 2 * t, :],
+                                     start=True, stop=False)
+                    nc.tensor.matmul(out=cps[:, i, :], lhsT=trig_t[:, 1, 4 * j + i, :], rhs=dmat[:, 2 * t + 1, :],
+                                     start=False, stop=True)
+                nc.scalar.copy(out=c_sb[:, 4 * j : 4 * j + 4, :], in_=cps[:])
                 banks.append(cps)
             return banks
 
@@ -133,18 +143,11 @@ def tile_groupqueryattention_pa_kernel(
         tab_k = const.tile([P, MT, 4 * HALF], F32, name="tab_k")
         c_q = const.tile([P, MT, DH], F32, name="c_q")
         c_k = const.tile([P, MT, DH], F32, name="c_k")
-        c_tmp = const.tile([P, MT, DH], F32, name="c_tmp")
-        for step in tab_steps(nc.vector, tab_q, 0):
+        for step in tab_steps(nc.gpsimd, tab_q, 0, 0, 2) + tab_steps(nc.gpsimd, tab_q, 0, 2, MT):
             step()
-        nc.vector.tensor_copy(out=shift2[:, :, 0:128], in_=bc4[:, :, 1, :])
-        nc.vector.tensor_scalar_mul(out=shift2[:, :, 128:192], in0=bc4[:, :, 1, 64:128], scalar1=-1.0)
-        nc.vector.tensor_copy(out=shift2[:, :, 192:256], in_=bc4[:, :, 1, 0:64])
-        for step in c_steps(nc.gpsimd, c_q, c_tmp, 0):
-            step()
-        cps_q = c_to_psum(c_q)
-        late_steps = tab_steps(nc.gpsimd, tab_k, 1) + c_steps(nc.gpsimd, c_k, c_tmp, 1)
+        late_steps = tab_steps(nc.gpsimd, tab_k, 1, 0, 4) + tab_steps(nc.gpsimd, tab_k, 1, 4, MT)
 
-        def prep(name, srcs, widths):
+        def prep(name, srcs, widths, share=False):
             rows = 256 * len(srcs)
             grouped = work.tile([P, 8 * rows], BF16, tag="grouped", bufs=3, name="grouped", align_bytes=64)
             gw = grouped[:].bitcast(F32)
@@ -162,10 +165,16 @@ def tile_groupqueryattention_pa_kernel(
                                 ident[:],
                             )
                     w0 = (g * rows + s * 256) * 2
-                    nc.scalar.copy(
-                        out=gw[:, w0 : w0 + 512].rearrange("p (r u) -> p r u", u=2),
-                        in_=tp[:].rearrange("p u r -> p r u"),
-                    )
+                    if share and g == 1:
+                        nc.vector.tensor_copy(
+                            out=gw[:, w0 : w0 + 512].rearrange("p (r u) -> p r u", u=2),
+                            in_=tp[:].rearrange("p u r -> p r u"),
+                        )
+                    else:
+                        nc.scalar.copy(
+                            out=gw[:, w0 : w0 + 512].rearrange("p (r u) -> p r u", u=2),
+                            in_=tp[:].rearrange("p u r -> p r u"),
+                        )
             for c0 in range(0, 2 * rows, widths):
                 nc.vector.quantize_mx(
                     out=codes[:, c0 : c0 + widths].bitcast(E5X4),
@@ -177,11 +186,11 @@ def tile_groupqueryattention_pa_kernel(
         xq = {}
         wqz = {}
 
-        def prep_x(pair, widths=512):
-            xq[pair] = prep("x%d" % pair, [x_sb[pair]], widths)
+        def prep_x(pair, widths=512, share=False):
+            xq[pair] = prep("x%d" % pair, [x_sb[pair]], widths, share)
 
-        def prep_w(key, widths=1024):
-            wqz[key] = prep("w" + key, w_sb[key], widths)
+        def prep_w(key, widths=1024, share=False):
+            wqz[key] = prep("w" + key, w_sb[key], widths, share)
 
         def mx_bank(m, key):
             acc = psum.tile([P, 512], F32, tag="acc", bufs=4, name="acc")
@@ -204,15 +213,8 @@ def tile_groupqueryattention_pa_kernel(
 
         state = {"late": 0}
 
-        def normed_bank(m, key, tab, cps, out, h0, group):
+        def normed_bank(m, key, tab, cps, c_sb, out, h0, group, offload):
             acc = mx_bank(m, key)
-            ss = work.tile([P, 4], F32, tag="ss", bufs=4, name="ss")
-            junk = work.tile([P, DH], F32, tag="junk", bufs=2, name="junk")
-            for h in range(4):
-                nc.scalar.activation(out=junk[:], in_=acc[:, h * DH : (h + 1) * DH], func=ACT.Square,
-                                     accum_out=ss[:, h : h + 1])
-            rinv = work.tile([P, 4], F32, tag="rinv", bufs=4, name="rinv")
-            nc.scalar.activation(out=rinv[:], in_=ss[:], func=ACT.Abs_reciprocal_sqrt, bias=EPS, scale=1.0 / DH)
             prod = work.tile([P, 4, 4 * HALF], F32, tag="prod", bufs=4, name="prod")
             nc.vector.tensor_tensor(
                 out=prod[:].rearrange("p h (k d) -> p h k d", k=2),
@@ -220,6 +222,13 @@ def tile_groupqueryattention_pa_kernel(
                 in1=acc[:].rearrange("p (h d) -> p h d", h=4).unsqueeze(2).to_broadcast([P, 4, 2, DH]),
                 op=ALU.mult,
             )
+            ss = work.tile([P, 4], F32, tag="ss", bufs=4, name="ss")
+            junk = work.tile([P, DH], F32, tag="junk", bufs=2, name="junk")
+            for h in range(4):
+                nc.scalar.activation(out=junk[:], in_=acc[:, h * DH : (h + 1) * DH], func=ACT.Square,
+                                     accum_out=ss[:, h : h + 1])
+            rinv = work.tile([P, 4], F32, tag="rinv", bufs=4, name="rinv")
+            nc.scalar.activation(out=rinv[:], in_=ss[:], func=ACT.Abs_reciprocal_sqrt, bias=EPS, scale=1.0 / DH)
             prod4 = prod[:].rearrange("p h (k e) -> p h k e", k=4)
             rot = work.tile([P, 4, DH], F32, tag="rot", bufs=4, name="rot")
             nc.gpsimd.tensor_tensor(
@@ -230,12 +239,19 @@ def tile_groupqueryattention_pa_kernel(
             if mm == 0:
                 state["o"] = work.tile([P, 4, group, DH], F32, tag="o", bufs=4, name="o")
             o = state["o"]
-            for h in range(4):
-                nc.vector.scalar_tensor_tensor(
-                    out=o[:, h, mm, :], in0=rot[:, h, :], scalar=rinv[:, h : h + 1],
-                    in1=cps[m // 4][:, (m % 4) * DH : (m % 4 + 1) * DH],
-                    op0=ALU.mult, op1=ALU.add,
-                )
+            if offload:
+                scaled = work.tile([P, 4, DH], F32, tag="scaled", bufs=3, name="scaled")
+                for h in range(4):
+                    nc.scalar.activation(out=scaled[:, h, :], in_=rot[:, h, :], func=ACT.Copy,
+                                         scale=rinv[:, h : h + 1])
+                nc.gpsimd.tensor_tensor(out=o[:, :, mm, :], in0=scaled[:],
+                                        in1=c_sb[:, m, :].unsqueeze(1).to_broadcast([P, 4, DH]), op=ALU.add)
+            else:
+                for h in range(4):
+                    nc.vector.scalar_tensor_tensor(
+                        out=o[:, h, mm, :], in0=rot[:, h, :], scalar=rinv[:, h : h + 1],
+                        in1=cps[m // 4][:, m % 4, :], op0=ALU.mult, op1=ALU.add,
+                    )
             if mm == group - 1:
                 nc.sync.dma_start(out=out_view(out, h0)[:, :, m - mm : m + 1, :], in_=o[:])
 
@@ -249,21 +265,25 @@ def tile_groupqueryattention_pa_kernel(
             if mm == 1:
                 nc.sync.dma_start(out=out_view(out_2, 0)[:, :, m - 1 : m + 1, :], in_=ov[:])
 
-        prep_x(0, 256)
-        prep_w("q0", 256)
+        prep_x(0, 256, True)
+        prep_w("q0", 256, True)
         prep_x(1)
+        trig_t = trig_transposed()
+        cps_q = c_tables(trig_t, 0, c_q)
         main = ["q0", "q1", "q2", "q3", "k"]
         extra = {(0, 1): lambda: prep_x(2), (0, 3): lambda: prep_x(3), (0, 4): lambda: prep_w("q1"),
                  (0, 6): lambda: prep_w("v")}
         cps_now = cps_q
         for ci, key in enumerate(main):
             if key == "k":
-                cps_now = c_to_psum(c_k)
+                cps_now = c_tables(trig_t, 1, c_k)
             for m in range(MT):
+                b = MT * ci + m
+                offload = b % OFFLOAD_EVERY == OFFLOAD_EVERY - 1 and b < 37
                 if key == "k":
-                    normed_bank(m, key, tab_k, cps_now, out_1, 0, 2 if m < 6 else 1)
+                    normed_bank(m, key, tab_k, cps_now, c_k, out_1, 0, 2 if m < 6 else 1, offload)
                 else:
-                    normed_bank(m, key, tab_q, cps_now, out_0, 4 * ci, 2)
+                    normed_bank(m, key, tab_q, cps_now, c_q, out_0, 4 * ci, 2, offload)
                 if (ci, m) in extra:
                     extra[(ci, m)]()
                 if ci >= 1 and m == 2 and ci + 1 < len(main):

@@ -87,21 +87,25 @@ def tile_groupqueryattention_pa_kernel(
         nc.tensor.matmul(out=bc_ps[:], lhsT=ones[:], rhs=vec_rows[:], start=True, stop=True)
         bc4 = bc_ps[:].rearrange("p (t s d) -> p t s d", t=2, s=2)
         gain4 = const.tile([P, 2, 4 * HALF], F32, name="gain4")
-        shift2 = const.tile([P, 2, 4 * HALF], F32, name="shift2")
+        vec2 = const.tile([P, 2, 2, 4 * HALF], F32, name="vec2")
         nc.vector.tensor_scalar_add(out=gain4[:, :, 0:64], in0=bc4[:, :, 0, 0:64], scalar1=1.0)
         nc.vector.tensor_scalar(
             out=gain4[:, :, 64:128], in0=bc4[:, :, 0, 64:128], scalar1=-1.0, scalar2=-1.0,
             op0=ALU.mult, op1=ALU.add,
         )
         nc.vector.tensor_scalar_add(out=gain4[:, :, 128:256], in0=bc4[:, :, 0, :], scalar1=1.0)
-        nc.vector.tensor_copy(out=shift2[:, :, 0:128], in_=bc4[:, :, 1, :])
-        nc.vector.tensor_scalar_mul(out=shift2[:, :, 128:192], in0=bc4[:, :, 1, 64:128], scalar1=-1.0)
-        nc.vector.tensor_copy(out=shift2[:, :, 192:256], in_=bc4[:, :, 1, 0:64])
-        dmat = const.tile([P, 4, DH], BF16, name="dmat")
+        nc.vector.tensor_copy(out=vec2[:, :, :, 0:128], in_=bc4[:, :, :, :])
+        nc.vector.tensor_scalar_mul(out=vec2[:, :, :, 128:192], in0=bc4[:, :, :, 64:128], scalar1=-1.0)
+        nc.vector.tensor_copy(out=vec2[:, :, :, 192:256], in_=bc4[:, :, :, 0:64])
+        dmat = const.tile([P, 8, DH], BF16, name="dmat")
         nc.vector.tensor_tensor(
-            out=dmat[:], in0=ident[:].unsqueeze(1).to_broadcast([P, 4, DH]),
-            in1=shift2[:].rearrange("p t (j d) -> p (t j) d", j=2), op=ALU.mult,
+            out=dmat[:], in0=ident[:].unsqueeze(1).to_broadcast([P, 8, DH]),
+            in1=vec2[:].rearrange("p t s (j d) -> p (t s j) d", j=2), op=ALU.mult,
         )
+        unit2 = const.tile([P, 2, DH], BF16, name="unit2")
+        nc.vector.tensor_copy(out=unit2[:, 0, :], in_=ident_bf[:])
+        nc.vector.tensor_scalar_mul(out=unit2[:, 1, 0:64], in0=ident_bf[:, 0:64], scalar1=-1.0)
+        nc.vector.tensor_copy(out=unit2[:, 1, 64:128], in_=ident_bf[:, 64:128])
 
         def over_m(ap, n_m):
             return ap.unsqueeze(1).to_broadcast([P, n_m, ap.shape[1]])
@@ -131,13 +135,24 @@ def tile_groupqueryattention_pa_kernel(
             for j in range(2):
                 cps = psum.tile([P, 4, DH], F32, tag="cps", bufs=2, name="cps")
                 for i in range(4):
-                    nc.tensor.matmul(out=cps[:, i, :], lhsT=trig_t[:, 0, 4 * j + i, :], rhs=dmat[:, 2 * t, :],
+                    nc.tensor.matmul(out=cps[:, i, :], lhsT=trig_t[:, 0, 4 * j + i, :], rhs=dmat[:, 4 * t + 2, :],
                                      start=True, stop=False)
-                    nc.tensor.matmul(out=cps[:, i, :], lhsT=trig_t[:, 1, 4 * j + i, :], rhs=dmat[:, 2 * t + 1, :],
+                    nc.tensor.matmul(out=cps[:, i, :], lhsT=trig_t[:, 1, 4 * j + i, :], rhs=dmat[:, 4 * t + 3, :],
                                      start=False, stop=True)
                 nc.scalar.copy(out=c_sb[:, 4 * j : 4 * j + 4, :], in_=cps[:])
                 banks.append(cps)
             return banks
+
+        def tab_k_pair(trig_t, m0):
+            tps = psum.tile([P, 2, 4 * HALF], F32, tag="tp", bufs=2, name="tabps")
+            for i in range(2):
+                out4 = tps[:, i, :].rearrange("p (k e) -> p k e", k=4)
+                for j, out_j in ((0, out4[:, 0:4:3, :]), (1, out4[:, 1:3, :])):
+                    nc.tensor.matmul(out=out_j, lhsT=trig_t[:, j, m0 + i, :],
+                                     rhs=unit2[:, j, :].rearrange("p (k e) -> p k e", k=2), start=True, stop=False)
+                    nc.tensor.matmul(out=out_j, lhsT=trig_t[:, j, m0 + i, :],
+                                     rhs=dmat[:, 4 + j, :].rearrange("p (k e) -> p k e", k=2), start=False, stop=True)
+            nc.scalar.copy(out=tab_k[:, m0 : m0 + 2, :], in_=tps[:])
 
         tab_q = const.tile([P, MT, 4 * HALF], F32, name="tab_q")
         tab_k = const.tile([P, MT, 4 * HALF], F32, name="tab_k")
@@ -145,7 +160,6 @@ def tile_groupqueryattention_pa_kernel(
         c_k = const.tile([P, MT, DH], F32, name="c_k")
         for step in tab_steps(nc.gpsimd, tab_q, 0, 0, 2) + tab_steps(nc.gpsimd, tab_q, 0, 2, MT):
             step()
-        late_steps = tab_steps(nc.gpsimd, tab_k, 1, 0, 4) + tab_steps(nc.gpsimd, tab_k, 1, 4, MT)
 
         def prep(name, srcs, widths, share=False):
             rows = 256 * len(srcs)
@@ -290,6 +304,6 @@ def tile_groupqueryattention_pa_kernel(
                     prep_w(main[ci + 1])
                 if ci >= 1 and m in (1, 5):
                     plain_bank(2 * (ci - 1) + (m - 1) // 4)
-                if m % 2 == 0 and (ci, m) >= (0, 2) and state["late"] < len(late_steps):
-                    late_steps[state["late"]]()
-                    state["late"] = state["late"] + 1
+                if ci in (1, 2) and m in (3, 7):
+                    tab_k_pair(trig_t, state["late"])
+                    state["late"] = state["late"] + 2

@@ -19,7 +19,7 @@ HALF = 64
 MT = SEQ // P
 EPS = 1e-6
 FLOPS = 2 * SEQ * KDIM * 3072
-OFFLOAD_EVERY = 6
+OFFLOAD_EVERY = 4
 
 
 def tile_groupqueryattention_pa_kernel(

@@ -229,22 +229,22 @@ def tile_groupqueryattention_pa_kernel(
 
         def normed_bank(m, key, tab, cps, c_sb, out, h0, group, offload):
             acc = mx_bank(m, key)
-            prod = work.tile([P, 4, 4 * HALF], F32, tag="prod", bufs=4, name="prod")
+            prod = work.tile([P, 4, 4 * HALF], F32, tag="prod", bufs=6, name="prod")
             nc.vector.tensor_tensor(
                 out=prod[:].rearrange("p h (k d) -> p h k d", k=2),
                 in0=tab[:, m, :].rearrange("p (k d) -> p k d", k=2).unsqueeze(1).to_broadcast([P, 4, 2, DH]),
                 in1=acc[:].rearrange("p (h d) -> p h d", h=4).unsqueeze(2).to_broadcast([P, 4, 2, DH]),
                 op=ALU.mult,
             )
-            ss = work.tile([P, 4], F32, tag="ss", bufs=4, name="ss")
+            ss = work.tile([P, 4], F32, tag="ss", bufs=6, name="ss")
             junk = work.tile([P, DH], F32, tag="junk", bufs=2, name="junk")
             for h in range(4):
                 nc.scalar.activation(out=junk[:], in_=acc[:, h * DH : (h + 1) * DH], func=ACT.Square,
                                      accum_out=ss[:, h : h + 1])
-            rinv = work.tile([P, 4], F32, tag="rinv", bufs=4, name="rinv")
+            rinv = work.tile([P, 4], F32, tag="rinv", bufs=6, name="rinv")
             nc.scalar.activation(out=rinv[:], in_=ss[:], func=ACT.Abs_reciprocal_sqrt, bias=EPS, scale=1.0 / DH)
             prod4 = prod[:].rearrange("p h (k e) -> p h k e", k=4)
-            rot = work.tile([P, 4, DH], F32, tag="rot", bufs=4, name="rot")
+            rot = work.tile([P, 4, DH], F32, tag="rot", bufs=6, name="rot")
             nc.gpsimd.tensor_tensor(
                 out=rot[:].rearrange("p h (t e) -> p h t e", t=2),
                 in0=prod4[:, :, 0:4:3, :], in1=prod4[:, :, 1:3, :], op=ALU.add,

from contextlib import ExitStack

import concourse.mybir as mybir
from concourse.masks import make_identity

F32 = mybir.dt.float32
BF16 = mybir.dt.bfloat16
U32 = mybir.dt.uint32
U8 = mybir.dt.uint8
E5X4 = mybir.dt.float8_e5m2_x4
ACT = mybir.ActivationFunctionType
ALU = mybir.AluOpType

P = 128
SEQ = 1024
KDIM = 1024
DH = 128
HALF = 64
MT = SEQ // P
EPS = 1e-6
FLOPS = 2 * SEQ * KDIM * 3072
OFFLOAD_EVERY = 4


def tile_groupqueryattention_pa_kernel(
    tc, x, sin_thetas, cos_thetas, wq, wk, wv, q_scale, q_shift, k_scale, k_shift, out_0, out_1, out_2
):
    nc = tc.nc
    with ExitStack() as ctx:
        const = ctx.enter_context(tc.tile_pool(name="const", bufs=1))
        work = ctx.enter_context(tc.tile_pool(name="work", bufs=1))
        psum = ctx.enter_context(tc.psum_pool(name="psum", bufs=1))

        vec_rows = const.tile([P, 4 * DH], BF16, name="vec_rows")
        nc.gpsimd.memset(vec_rows[:], 0.0)
        for j, vec in enumerate((q_scale, q_shift, k_scale, k_shift)):
            nc.sync.dma_start(
                out=vec_rows[0:1, j * DH : (j + 1) * DH], in_=vec.rearrange("(o d) -> o d", o=1)
            )
        cos_sb = const.tile([P, MT, DH], BF16, name="cos_sb")
        sin_sb = const.tile([P, MT, DH], BF16, name="sin_sb")

        x_view = x[0].rearrange("(p m) k -> p m k", m=MT)
        x_sb = []
        w_sb = {}

        def load_x(pair):
            t = const.tile([P, 2, KDIM], BF16, name="x_sb%d" % pair)
            nc.sync.dma_start(out=t[:], in_=x_view[:, 2 * pair : 2 * pair + 2, :])
            x_sb.append(t)

        def load_w(key, w, row0):
            halves = []
            for hf in range(2):
                t = const.tile([P, 2, KDIM], BF16, name="w_sb_%s_%d" % (key, hf))
                nc.sync.dma_start(
                    out=t[:],
                    in_=w[row0 + 256 * hf : row0 + 256 * (hf + 1), :].rearrange("(c p) k -> p c k", p=P),
                )
                halves.append(t)
            w_sb[key] = halves

        load_x(0)
        load_w("q0", wq, 0)
        nc.sync.dma_start(out=cos_sb[:], in_=cos_thetas.rearrange("(p m) d -> p m d", m=MT))
        nc.sync.dma_start(out=sin_sb[:], in_=sin_thetas.rearrange("(p m) d -> p m d", m=MT))
        load_x(1)
        load_x(2)
        load_x(3)
        load_w("v", wv, 0)
        load_w("q1", wq, 512)
        load_w("q2", wq, 1024)
        load_w("q3", wq, 1536)
        load_w("k", wk, 0)

        ident = const.tile([P, P], F32, name="ident")
        make_identity(nc, ident[:])
        ident_bf = const.tile([P, P], BF16, name="ident_bf")
        make_identity(nc, ident_bf[:])
        ones = const.tile([P, P], BF16, name="ones")
        nc.vector.memset(ones[:], 1.0)
        warm = const.tile([P, 1], F32, name="warm")
        nc.vector.memset(warm[:], 1.0)
        nc.scalar.activation(out=warm[:], in_=warm[:], func=ACT.Abs_reciprocal_sqrt)

        bc_ps = psum.tile([P, 512], F32, tag="tp", bufs=2, name="bc_ps")
        nc.tensor.matmul(out=bc_ps[:], lhsT=ones[:], rhs=vec_rows[:], start=True, stop=True)
        bc4 = bc_ps[:].rearrange("p (t s d) -> p t s d", t=2, s=2)
        gain4 = const.tile([P, 2, 4 * HALF], F32, name="gain4")
        vec2 = const.tile([P, 2, 2, 4 * HALF], F32, name="vec2")
        nc.vector.tensor_scalar_add(out=gain4[:, :, 0:64], in0=bc4[:, :, 0, 0:64], scalar1=1.0)
        nc.vector.tensor_scalar(
            out=gain4[:, :, 64:128], in0=bc4[:, :, 0, 64:128], scalar1=-1.0, scalar2=-1.0,
            op0=ALU.mult, op1=ALU.add,
        )
        nc.vector.tensor_scalar_add(out=gain4[:, :, 128:256], in0=bc4[:, :, 0, :], scalar1=1.0)
        nc.vector.tensor_copy(out=vec2[:, :, :, 0:128], in_=bc4[:, :, :, :])
        nc.vector.tensor_scalar_mul(out=vec2[:, :, :, 128:192], in0=bc4[:, :, :, 64:128], scalar1=-1.0)
        nc.vector.tensor_copy(out=vec2[:, :, :, 192:256], in_=bc4[:, :, :, 0:64])
        dmat = const.tile([P, 8, DH], BF16, name="dmat")
        nc.vector.tensor_tensor(
            out=dmat[:], in0=ident[:].unsqueeze(1).to_broadcast([P, 8, DH]),
            in1=vec2[:].rearrange("p t s (j d) -> p (t s j) d", j=2), op=ALU.mult,
        )
        unit2 = const.tile([P, 2, DH], BF16, name="unit2")
        nc.vector.tensor_copy(out=unit2[:, 0, :], in_=ident_bf[:])
        nc.vector.tensor_scalar_mul(out=unit2[:, 1, 0:64], in0=ident_bf[:, 0:64], scalar1=-1.0)
        nc.vector.tensor_copy(out=unit2[:, 1, 64:128], in_=ident_bf[:, 64:128])

        def over_m(ap, n_m):
            return ap.unsqueeze(1).to_broadcast([P, n_m, ap.shape[1]])

        def tab_steps(eng, tab, t, m0, m1):
            ms = slice(m0, m1)
            return [
                lambda: eng.tensor_tensor(out=tab[:, ms, 0:64], in0=cos_sb[:, ms, 0:64],
                                          in1=over_m(gain4[:, t, 0:64], m1 - m0), op=ALU.mult),
                lambda: eng.tensor_tensor(out=tab[:, ms, 64:192], in0=sin_sb[:, ms, :],
                                          in1=over_m(gain4[:, t, 64:192], m1 - m0), op=ALU.mult),
                lambda: eng.tensor_tensor(out=tab[:, ms, 192:256], in0=cos_sb[:, ms, 64:128],
                                          in1=over_m(gain4[:, t, 192:256], m1 - m0), op=ALU.mult),
            ]

        def trig_transposed():
            trig_t = const.tile([P, 2, MT, P], BF16, name="trig_t")
            for j, src in enumerate((cos_sb, sin_sb)):
                tps = psum.tile([P, MT, P], BF16, tag="acc", bufs=4, name="tps")
                for m in range(MT):
                    nc.tensor.transpose(tps[:, m, :], src[:, m, :], ident_bf[:])
                nc.scalar.copy(out=trig_t[:, j, :, :], in_=tps[:])
            return trig_t

        def c_tables(trig_t, t, c_sb):
            banks = []
            for j in range(2):
                cps = psum.tile([P, 4, DH], F32, tag="cps", bufs=2, name="cps")
                for i in range(4):
                    nc.tensor.matmul(out=cps[:, i, :], lhsT=trig_t[:, 0, 4 * j + i, :], rhs=dmat[:, 4 * t + 2, :],
                                     start=True, stop=False)
                    nc.tensor.matmul(out=cps[:, i, :], lhsT=trig_t[:, 1, 4 * j + i, :], rhs=dmat[:, 4 * t + 3, :],
                                     start=False, stop=True)
                nc.scalar.copy(out=c_sb[:, 4 * j : 4 * j + 4, :], in_=cps[:])
                banks.append(cps)
            return banks

        def tab_k_pair(trig_t, m0):
            tps = psum.tile([P, 2, 4 * HALF], F32, tag="tp", bufs=2, name="tabps")
            for i in range(2):
                out4 = tps[:, i, :].rearrange("p (k e) -> p k e", k=4)
                for j, out_j in ((0, out4[:, 0:4:3, :]), (1, out4[:, 1:3, :])):
                    nc.tensor.matmul(out=out_j, lhsT=trig_t[:, j, m0 + i, :],
                                     rhs=unit2[:, j, :].rearrange("p (k e) -> p k e", k=2), start=True, stop=False)
                    nc.tensor.matmul(out=out_j, lhsT=trig_t[:, j, m0 + i, :],
                                     rhs=dmat[:, 4 + j, :].rearrange("p (k e) -> p k e", k=2), start=False, stop=True)
            nc.scalar.copy(out=tab_k[:, m0 : m0 + 2, :], in_=tps[:])

        tab_q = const.tile([P, MT, 4 * HALF], F32, name="tab_q")
        tab_k = const.tile([P, MT, 4 * HALF], F32, name="tab_k")
        c_q = const.tile([P, MT, DH], F32, name="c_q")
        c_k = const.tile([P, MT, DH], F32, name="c_k")
        for step in tab_steps(nc.gpsimd, tab_q, 0, 0, 2) + tab_steps(nc.gpsimd, tab_q, 0, 2, MT):
            step()

        def prep(name, srcs, widths, share=False):
            rows = 256 * len(srcs)
            grouped = work.tile([P, 8 * rows], BF16, tag="grouped", bufs=3, name="grouped", align_bytes=64)
            gw = grouped[:].bitcast(F32)
            codes = const.tile([P, 2 * rows], U32, name="codes_" + name, align_bytes=64)
            scales = const.tile([P, 2 * rows], U8, name="scales_" + name, align_bytes=64)
            for s, src in enumerate(srcs):
                for g in range(2):
                    tp = psum.tile([P, 2, 256], F32, tag="tp", bufs=2, name="tp")
                    for c in range(2):
                        words = src[:, c, :].bitcast(F32)
                        for u in range(2):
                            nc.tensor.transpose(
                                tp[:, u, c * P : (c + 1) * P],
                                words[:, 256 * g + u : 256 * (g + 1) : 2],
                                ident[:],
                            )
                    w0 = (g * rows + s * 256) * 2
                    if share and g == 1:
                        nc.vector.tensor_copy(
                            out=gw[:, w0 : w0 + 512].rearrange("p (r u) -> p r u", u=2),
                            in_=tp[:].rearrange("p u r -> p r u"),
                        )
                    else:
                        nc.scalar.copy(
                            out=gw[:, w0 : w0 + 512].rearrange("p (r u) -> p r u", u=2),
                            in_=tp[:].rearrange("p u r -> p r u"),
                        )
            for c0 in range(0, 2 * rows, widths):
                nc.vector.quantize_mx(
                    out=codes[:, c0 : c0 + widths].bitcast(E5X4),
                    scales=scales[:, c0 : c0 + widths],
                    in_=grouped[:, 4 * c0 : 4 * (c0 + widths)],
                )
            return codes, scales

        xq = {}
        wqz = {}

        def prep_x(pair, widths=512, share=False):
            xq[pair] = prep("x%d" % pair, [x_sb[pair]], widths, share)

        def prep_w(key, widths=1024, share=False):
            wqz[key] = prep("w" + key, w_sb[key], widths, share)

        def mx_bank(m, key):
            acc = psum.tile([P, 512], F32, tag="acc", bufs=4, name="acc")
            pair, half = divmod(m, 2)
            xc, xs = xq[pair]
            wc, ws = wqz[key]
            for g in range(2):
                xcols = slice(g * 256 + half * P, g * 256 + (half + 1) * P)
                wcols = slice(g * 512, (g + 1) * 512)
                nc.tensor.matmul_mx(
                    out=acc[:],
                    lhsT=xc[:, xcols].bitcast(E5X4), lhsT_scale=xs[:, xcols],
                    rhs=wc[:, wcols].bitcast(E5X4), rhs_scale=ws[:, wcols],
                    start=(g == 0), stop=(g == 1),
                )
            return acc

        def out_view(out, h0):
            return out[0, h0 : h0 + 4, :, :].rearrange("h (p m) d -> p h m d", m=MT)

        state = {"late": 0}

        def normed_bank(m, key, tab, cps, c_sb, out, h0, group, offload):
            acc = mx_bank(m, key)
            prod = work.tile([P, 4, 4 * HALF], F32, tag="prod", bufs=6, name="prod")
            nc.vector.tensor_tensor(
                out=prod[:].rearrange("p h (k d) -> p h k d", k=2),
                in0=tab[:, m, :].rearrange("p (k d) -> p k d", k=2).unsqueeze(1).to_broadcast([P, 4, 2, DH]),
                in1=acc[:].rearrange("p (h d) -> p h d", h=4).unsqueeze(2).to_broadcast([P, 4, 2, DH]),
                op=ALU.mult,
            )
            ss = work.tile([P, 4], F32, tag="ss", bufs=6, name="ss")
            junk = work.tile([P, DH], F32, tag="junk", bufs=2, name="junk")
            for h in range(4):
                nc.scalar.activation(out=junk[:], in_=acc[:, h * DH : (h + 1) * DH], func=ACT.Square,
                                     accum_out=ss[:, h : h + 1])
            rinv = work.tile([P, 4], F32, tag="rinv", bufs=6, name="rinv")
            nc.scalar.activation(out=rinv[:], in_=ss[:], func=ACT.Abs_reciprocal_sqrt, bias=EPS, scale=1.0 / DH)
            prod4 = prod[:].rearrange("p h (k e) -> p h k e", k=4)
            rot = work.tile([P, 4, DH], F32, tag="rot", bufs=6, name="rot")
            nc.gpsimd.tensor_tensor(
                out=rot[:].rearrange("p h (t e) -> p h t e", t=2),
                in0=prod4[:, :, 0:4:3, :], in1=prod4[:, :, 1:3, :], op=ALU.add,
            )
            mm = m % group
            if mm == 0:
                state["o"] = work.tile([P, 4, group, DH], F32, tag="o", bufs=4, name="o")
            o = state["o"]
            if offload:
                scaled = work.tile([P, 4, DH], F32, tag="scaled", bufs=3, name="scaled")
                for h in range(4):
                    nc.scalar.activation(out=scaled[:, h, :], in_=rot[:, h, :], func=ACT.Copy,
                                         scale=rinv[:, h : h + 1])
                nc.gpsimd.tensor_tensor(out=o[:, :, mm, :], in0=scaled[:],
                                        in1=c_sb[:, m, :].unsqueeze(1).to_broadcast([P, 4, DH]), op=ALU.add)
            else:
                for h in range(4):
                    nc.vector.scalar_tensor_tensor(
                        out=o[:, h, mm, :], in0=rot[:, h, :], scalar=rinv[:, h : h + 1],
                        in1=cps[m // 4][:, m % 4, :], op0=ALU.mult, op1=ALU.add,
                    )
            if mm == group - 1:
                nc.sync.dma_start(out=out_view(out, h0)[:, :, m - mm : m + 1, :], in_=o[:])

        def plain_bank(m):
            acc = mx_bank(m, "v")
            mm = m % 2
            if mm == 0:
                state["ov"] = work.tile([P, 4, 2, DH], F32, tag="ov", bufs=2, name="ov")
            ov = state["ov"]
            nc.scalar.copy(out=ov[:, :, mm, :], in_=acc[:].rearrange("p (h d) -> p h d", h=4))
            if mm == 1:
                nc.sync.dma_start(out=out_view(out_2, 0)[:, :, m - 1 : m + 1, :], in_=ov[:])

        prep_x(0, 256, True)
        prep_w("q0", 256, True)
        prep_x(1)
        trig_t = trig_transposed()
        cps_q = c_tables(trig_t, 0, c_q)
        main = ["q0", "q1", "q2", "q3", "k"]
        extra = {(0, 1): lambda: prep_x(2), (0, 3): lambda: prep_x(3), (0, 4): lambda: prep_w("q1"),
                 (0, 6): lambda: prep_w("v")}
        cps_now = cps_q
        for ci, key in enumerate(main):
            if key == "k":
                cps_now = c_tables(trig_t, 1, c_k)
            for m in range(MT):
                b = MT * ci + m
                offload = b % OFFLOAD_EVERY == OFFLOAD_EVERY - 1 and b < 37
                if key == "k":
                    normed_bank(m, key, tab_k, cps_now, c_k, out_1, 0, 2 if m < 6 else 1, offload)
                else:
                    normed_bank(m, key, tab_q, cps_now, c_q, out_0, 4 * ci, 2, offload)
                if (ci, m) in extra:
                    extra[(ci, m)]()
                if ci >= 1 and m == 2 and ci + 1 < len(main):
                    prep_w(main[ci + 1])
                if ci >= 1 and m in (1, 5):
                    plain_bank(2 * (ci - 1) + (m - 1) // 4)
                if ci in (1, 2) and m in (3, 7):
                    tab_k_pair(trig_t, state["late"])
                    state["late"] = state["late"] + 2
